import numpy as np
import ml_dtypes


def mxq(x, axis, fmt="e4m3"):
    dtype, down = {"e4m3": (ml_dtypes.float8_e4m3fn, 7), "e5m2": (ml_dtypes.float8_e5m2, 14)}[fmt]
    v = np.moveaxis(np.asarray(x, np.float32).astype(ml_dtypes.bfloat16).astype(np.float64), axis, -1)
    blocks = v.reshape(v.shape[:-1] + (-1, 32))
    amax = np.abs(blocks).max(-1, keepdims=True)
    byte = np.maximum(np.where(amax > 0, np.frexp(amax)[1] - 1 + 127, 0) - down, 1)
    scale = np.exp2(byte - 127.0)
    codes = (blocks / scale).astype(np.float32).astype(dtype).astype(np.float64)
    return np.moveaxis((codes * scale).reshape(v.shape), -1, axis)


WIDE = False


def mx_kscale(k):
    if not WIDE:
        return np.ones(k)
    levels = np.array([10, -10, 5, -5, 0])
    a = np.random.permutation(np.resize(levels, k // 512 * 4)).reshape(k // 512, 4)
    idx = np.arange(k)
    return np.exp2(a[idx // 512, idx % 128 // 32])


BF16 = ml_dtypes.bfloat16


def bf(x):
    return np.asarray(x, np.float32).astype(BF16)


def f64(x):
    return np.asarray(x).astype(np.float64)


B, S, H, NH, HD = 4, 4096, 512, 1, 128
E = NH * HD


def heads(t):
    return t.reshape(B, S, NH, HD).transpose(0, 2, 1, 3)


def setup_inputs():
    s = mx_kscale(H)
    c = S ** -0.25
    return {"hidden_states": bf(np.random.standard_normal((B, S, H)) * s),
            "Wk": bf(np.random.standard_normal((H, E)) * c / np.sqrt(H) / s[:, None]),
            "bk": bf(np.random.standard_normal(E) / np.sqrt(S)),
            "Wv": bf(np.random.standard_normal((H, E)) * c / np.sqrt(H) / s[:, None]),
            "bv": bf(np.random.standard_normal(E) / np.sqrt(S))}


def reference(hidden_states, Wk, bk, Wv, bv):
    xq = mxq(f64(hidden_states), 2, "e4m3")
    k = heads((xq @ mxq(f64(Wk), 0, "e4m3")) + f64(bk))
    v = heads((xq @ mxq(f64(Wv), 0, "e4m3")) + f64(bv))
    return mxq(k, 2, "e4m3").transpose(0, 1, 3, 2) @ mxq(v, 2, "e4m3")

@@ -1,0 +1,193 @@
+from contextlib import ExitStack
+
+import concourse.mybir as mybir
+from concourse.masks import make_identity
+
+BF16 = mybir.dt.bfloat16
+F32 = mybir.dt.float32
+U32 = mybir.dt.uint32
+U8 = mybir.dt.uint8
+FP8X4 = mybir.dt.float8_e4m3fn_x4
+
+P = 128
+PACK = 4
+K_PASS = P * PACK
+
+B, S, H, E = 4, 4096, 512, 128
+CHUNK = K_PASS
+CHUNKS_PER_BATCH = S // CHUNK
+N_CHUNKS = B * CHUNKS_PER_BATCH
+H_WORDS = H // 2
+
+FLOPS = 2 * B * S * H * 2 * E + 2 * B * S * E * E
+
+LAG_QUANTISE_X = 2
+LAG_PROJECT = 3
+LAG_BIAS = 4
+LAG_STATE = 5
+
+
+def tile_linearattention_pa_t_kernel(tc, hidden_states, Wk, bk, Wv, bv, out):
+    nc = tc.nc
+    assert H == K_PASS, "the first contraction is exactly one matmul_mx pass"
+    x_rows = hidden_states.flatten_outer_dims()
+
+    with ExitStack() as ctx:
+        const = ctx.enter_context(tc.tile_pool(name="const", bufs=1))
+        x_pool = ctx.enter_context(tc.tile_pool(name="x", bufs=N_CHUNKS))
+        work = ctx.enter_context(tc.tile_pool(name="work", bufs=3))
+        xt_psum = ctx.enter_context(tc.psum_pool(name="xt_psum", bufs=4))
+        proj_psum = ctx.enter_context(tc.psum_pool(name="proj_psum", bufs=3))
+        state_psum = ctx.enter_context(tc.psum_pool(name="state_psum", bufs=1))
+        ctx.enter_context(tc.manual_schedule())
+
+        w_raw = const.tile([P, 2, PACK, E], BF16)
+        for side, w in enumerate((Wk, Wv)):
+            nc.sync.dma_start(
+                out=w_raw[:, side].rearrange("q (u e) n -> q u e n", u=2),
+                in_=w.rearrange("(u q e) n -> q u e n", u=2, e=2),
+            )
+        bias_rows = const.tile([P, 2, E], BF16)
+        nc.vector.memset(bias_rows[:], 0.0)
+        for side, bias in enumerate((bk, bv)):
+            nc.sync.dma_start(
+                out=bias_rows[0:1, side, :], in_=bias.rearrange("(o n) -> o n", o=1)
+            )
+        x_chunks = []
+        for c in range(N_CHUNKS):
+            x_chunk = x_pool.tile([P, PACK * H], BF16)
+            nc.sync.dma_start(
+                out=x_chunk[:],
+                in_=x_rows[c * CHUNK : (c + 1) * CHUNK, :].rearrange("(m j) h -> m (j h)", j=PACK),
+            )
+            x_chunks.append(x_chunk)
+
+        ones = const.tile([P, P], BF16)
+        nc.vector.memset(ones[:], 1.0)
+        identity = const.tile([P, P], F32)
+        make_identity(nc, identity[:])
+
+        w_grouped = const.tile([P, 2, E, PACK], BF16, align_bytes=64)
+        nc.vector.tensor_copy(out=w_grouped[:], in_=w_raw[:].rearrange("q s t n -> q s n t"))
+
+        bias_bank = proj_psum.tile([P, 2, E], F32, tag="proj")
+        nc.tensor.matmul(
+            out=bias_bank[:].rearrange("m s n -> m (s n)"),
+            lhsT=ones[:],
+            rhs=bias_rows[:].rearrange("r s n -> r (s n)"),
+            start=True,
+            stop=True,
+        )
+        bias_all = const.tile([P, 2, E], F32)
+        nc.vector.tensor_copy(out=bias_all[:], in_=bias_bank[:])
+
+        w_codes = const.tile([P, 2 * E], U32, align_bytes=64)
+        w_scales = const.tile([P, 2 * E], U8, align_bytes=64)
+        nc.vector.quantize_mx(
+            out=w_codes[:].bitcast(FP8X4),
+            scales=w_scales[:],
+            in_=w_grouped[:].rearrange("q s n t -> q (s n t)"),
+        )
+
+        state = state_psum.tile([P, B, E], F32)
+
+        x_grouped = {}
+        x_quantised = {}
+        projections = {}
+        kv_grouped = {}
+        kv_quantised = {}
+
+        def transpose_x(c):
+            words = x_chunks[c][:].bitcast(F32)
+            grouped = work.tile([P, PACK * P * PACK], BF16, align_bytes=64, tag="x_grouped")
+            grouped_words = grouped[:].bitcast(F32).rearrange("q (j m u) -> q j m u", j=PACK, u=2)
+            for half in range(2):
+                xt = xt_psum.tile([P, 2, 2, P], F32)
+                for j2 in range(2):
+                    for u in range(2):
+                        first = (2 * half + j2) * H_WORDS + u * P
+                        nc.tensor.transpose(xt[:, j2, u, :], words[:, first : first + P], identity[:])
+                nc.scalar.copy(
+                    out=grouped_words[:, 2 * half : 2 * half + 2],
+                    in_=xt[:].rearrange("q j u m -> q j m u"),
+                )
+            x_grouped[c] = grouped
+
+        def quantise_x(c):
+            codes = work.tile([P, PACK * P], U32, align_bytes=64, tag="x_codes")
+            scales = work.tile([P, PACK * P], U8, align_bytes=64, tag="x_scales")
+            nc.vector.quantize_mx(out=codes[:].bitcast(FP8X4), scales=scales[:], in_=x_grouped[c][:])
+            x_quantised[c] = (codes, scales)
+
+        def project(c):
+            codes, scales = x_quantised[c]
+            banks = []
+            for side in range(2):
+                proj = proj_psum.tile([P, PACK, E], F32)
+                for j in range(PACK):
+                    nc.tensor.matmul_mx(
+                        out=proj[:, j, :],
+                        lhsT=codes[:, j * P : (j + 1) * P].bitcast(FP8X4),
+                        lhsT_scale=scales[:, j * P : (j + 1) * P],
+                        rhs=w_codes[:, side * E : (side + 1) * E].bitcast(FP8X4),
+                        rhs_scale=w_scales[:, side * E : (side + 1) * E],
+                        start=True,
+                        stop=True,
+                    )
+                banks.append(proj)
+            projections[c] = banks
+
+        def add_bias(c):
+            grouped = work.tile([P, 2, E, PACK], BF16, align_bytes=64, tag="kv_grouped")
+            for side in range(2):
+                nc.vector.tensor_tensor(
+                    out=grouped[:, side],
+                    in0=projections[c][side][:].rearrange("m j n -> m n j"),
+                    in1=bias_all[:, side, :].unsqueeze(2).to_broadcast([P, E, PACK]),
+                    op=mybir.AluOpType.add,
+                )
+            kv_grouped[c] = grouped
+
+        def quantise_kv(c):
+            codes = work.tile([P, 2 * E], U32, align_bytes=64, tag="kv_codes")
+            scales = work.tile([P, 2 * E], U8, align_bytes=64, tag="kv_scales")
+            nc.vector.quantize_mx(
+                out=codes[:].bitcast(FP8X4),
+                scales=scales[:],
+                in_=kv_grouped[c][:].rearrange("m s n j -> m (s n j)"),
+            )
+            kv_quantised[c] = (codes, scales)
+
+        def add_to_state(c):
+            codes, scales = kv_quantised[c]
+            b, i = divmod(c, CHUNKS_PER_BATCH)
+            nc.tensor.matmul_mx(
+                out=state[:, b, :],
+                lhsT=codes[:, 0:E].bitcast(FP8X4),
+                lhsT_scale=scales[:, 0:E],
+                rhs=codes[:, E : 2 * E].bitcast(FP8X4),
+                rhs_scale=scales[:, E : 2 * E],
+                start=(i == 0),
+                stop=(i == CHUNKS_PER_BATCH - 1),
+            )
+
+        def in_range(c):
+            return 0 <= c < N_CHUNKS
+
+        for t in range(N_CHUNKS + LAG_STATE):
+            if in_range(t - LAG_BIAS):
+                add_bias(t - LAG_BIAS)
+            if in_range(t - LAG_PROJECT):
+                project(t - LAG_PROJECT)
+            if in_range(t - LAG_QUANTISE_X):
+                quantise_x(t - LAG_QUANTISE_X)
+            if in_range(t - LAG_BIAS):
+                quantise_kv(t - LAG_BIAS)
+            if in_range(t - LAG_STATE):
+                add_to_state(t - LAG_STATE)
+            if in_range(t):
+                transpose_x(t)
+
+        result = const.tile([P, B, E], F32)
+        nc.vector.tensor_copy(out=result[:], in_=state[:])
+        nc.sync.dma_start(out=out.rearrange("b o d e -> d (b o) e"), in_=result[:])

@@ -8,6 +8,7 @@ F32 = mybir.dt.float32
 U32 = mybir.dt.uint32
 U8 = mybir.dt.uint8
 FP8X4 = mybir.dt.float8_e4m3fn_x4
+ADD = mybir.AluOpType.add
 
 P = 128
 PACK = 4
@@ -18,13 +19,16 @@ CHUNK = K_PASS
 CHUNKS_PER_BATCH = S // CHUNK
 N_CHUNKS = B * CHUNKS_PER_BATCH
 H_WORDS = H // 2
+K_SIDE, V_SIDE = 0, 1
 
 FLOPS = 2 * B * S * H * 2 * E + 2 * B * S * E * E
 
-LAG_QUANTISE_X = 2
-LAG_PROJECT = 3
-LAG_BIAS = 4
-LAG_STATE = 5
+ROUND = 2
+N_ROUNDS = N_CHUNKS // ROUND
+LAG_QUANTISE_X = 1
+LAG_PROJECT = 2
+LAG_BIAS = 3
+LAG_STATE = 4
 
 
 def tile_linearattention_pa_t_kernel(tc, hidden_states, Wk, bk, Wv, bv, out):
@@ -35,21 +39,22 @@ def tile_linearattention_pa_t_kernel(tc, hidden_states, Wk, bk, Wv, bv, out):
     with ExitStack() as ctx:
         const = ctx.enter_context(tc.tile_pool(name="const", bufs=1))
         x_pool = ctx.enter_context(tc.tile_pool(name="x", bufs=N_CHUNKS))
-        work = ctx.enter_context(tc.tile_pool(name="work", bufs=3))
-        xt_psum = ctx.enter_context(tc.psum_pool(name="xt_psum", bufs=4))
-        proj_psum = ctx.enter_context(tc.psum_pool(name="proj_psum", bufs=3))
+        by_chunk = ctx.enter_context(tc.tile_pool(name="by_chunk", bufs=2 * ROUND))
+        by_round = ctx.enter_context(tc.tile_pool(name="by_round", bufs=2))
+        xt_psum = ctx.enter_context(tc.psum_pool(name="xt_psum", bufs=3))
+        proj_psum = ctx.enter_context(tc.psum_pool(name="proj_psum", bufs=4))
         state_psum = ctx.enter_context(tc.psum_pool(name="state_psum", bufs=1))
         ctx.enter_context(tc.manual_schedule())
 
         w_raw = const.tile([P, 2, PACK, E], BF16)
-        for side, w in enumerate((Wk, Wv)):
+        for side, w in ((K_SIDE, Wk), (V_SIDE, Wv)):
             nc.sync.dma_start(
                 out=w_raw[:, side].rearrange("q (u e) n -> q u e n", u=2),
                 in_=w.rearrange("(u q e) n -> q u e n", u=2, e=2),
             )
         bias_rows = const.tile([P, 2, E], BF16)
         nc.vector.memset(bias_rows[:], 0.0)
-        for side, bias in enumerate((bk, bv)):
+        for side, bias in ((K_SIDE, bk), (V_SIDE, bv)):
             nc.sync.dma_start(
                 out=bias_rows[0:1, side, :], in_=bias.rearrange("(o n) -> o n", o=1)
             )
@@ -78,8 +83,10 @@ def tile_linearattention_pa_t_kernel(tc, hidden_states, Wk, bk, Wv, bv, out):
             start=True,
             stop=True,
         )
-        bias_all = const.tile([P, 2, E], F32)
-        nc.vector.tensor_copy(out=bias_all[:], in_=bias_bank[:])
+        bias_grouped = const.tile([P, 2, E, PACK], F32)
+        nc.vector.tensor_copy(
+            out=bias_grouped[:], in_=bias_bank[:].unsqueeze(3).to_broadcast([P, 2, E, PACK])
+        )
 
         w_codes = const.tile([P, 2 * E], U32, align_bytes=64)
         w_scales = const.tile([P, 2 * E], U8, align_bytes=64)
@@ -94,12 +101,19 @@ def tile_linearattention_pa_t_kernel(tc, hidden_states, Wk, bk, Wv, bv, out):
         x_grouped = {}
         x_quantised = {}
         projections = {}
+        detour_sums = {}
         kv_grouped = {}
         kv_quantised = {}
 
+        def chunks_of(r):
+            return range(r * ROUND, (r + 1) * ROUND)
+
+        def takes_detour(c, side):
+            return c % ROUND == ROUND - 1 and side == V_SIDE
+
         def transpose_x(c):
             words = x_chunks[c][:].bitcast(F32)
-            grouped = work.tile([P, PACK * P * PACK], BF16, align_bytes=64, tag="x_grouped")
+            grouped = by_chunk.tile([P, PACK * P * PACK], BF16, align_bytes=64, tag="x_grouped")
             grouped_words = grouped[:].bitcast(F32).rearrange("q (j m u) -> q j m u", j=PACK, u=2)
             for half in range(2):
                 xt = xt_psum.tile([P, 2, 2, P], F32)
@@ -114,79 +128,98 @@ def tile_linearattention_pa_t_kernel(tc, hidden_states, Wk, bk, Wv, bv, out):
             x_grouped[c] = grouped
 
         def quantise_x(c):
-            codes = work.tile([P, PACK * P], U32, align_bytes=64, tag="x_codes")
-            scales = work.tile([P, PACK * P], U8, align_bytes=64, tag="x_scales")
+            codes = by_chunk.tile([P, PACK * P], U32, align_bytes=64, tag="x_codes")
+            scales = by_chunk.tile([P, PACK * P], U8, align_bytes=64, tag="x_scales")
             nc.vector.quantize_mx(out=codes[:].bitcast(FP8X4), scales=scales[:], in_=x_grouped[c][:])
             x_quantised[c] = (codes, scales)
 
-        def project(c):
+        def project(c, side):
             codes, scales = x_quantised[c]
-            banks = []
-            for side in range(2):
-                proj = proj_psum.tile([P, PACK, E], F32)
-                for j in range(PACK):
-                    nc.tensor.matmul_mx(
-                        out=proj[:, j, :],
-                        lhsT=codes[:, j * P : (j + 1) * P].bitcast(FP8X4),
-                        lhsT_scale=scales[:, j * P : (j + 1) * P],
-                        rhs=w_codes[:, side * E : (side + 1) * E].bitcast(FP8X4),
-                        rhs_scale=w_scales[:, side * E : (side + 1) * E],
-                        start=True,
-                        stop=True,
-                    )
-                banks.append(proj)
-            projections[c] = banks
-
-        def add_bias(c):
-            grouped = work.tile([P, 2, E, PACK], BF16, align_bytes=64, tag="kv_grouped")
-            for side in range(2):
-                nc.vector.tensor_tensor(
-                    out=grouped[:, side],
-                    in0=projections[c][side][:].rearrange("m j n -> m n j"),
-                    in1=bias_all[:, side, :].unsqueeze(2).to_broadcast([P, E, PACK]),
-                    op=mybir.AluOpType.add,
+            proj = proj_psum.tile([P, PACK, E], F32)
+            for j in range(PACK):
+                nc.tensor.matmul_mx(
+                    out=proj[:, j, :],
+                    lhsT=codes[:, j * P : (j + 1) * P].bitcast(FP8X4),
+                    lhsT_scale=scales[:, j * P : (j + 1) * P],
+                    rhs=w_codes[:, side * E : (side + 1) * E].bitcast(FP8X4),
+                    rhs_scale=w_scales[:, side * E : (side + 1) * E],
+                    start=True,
+                    stop=True,
                 )
-            kv_grouped[c] = grouped
+            projections[c, side] = proj
 
-        def quantise_kv(c):
-            codes = work.tile([P, 2 * E], U32, align_bytes=64, tag="kv_codes")
-            scales = work.tile([P, 2 * E], U8, align_bytes=64, tag="kv_scales")
+        def project_round(r):
+            banks = [(c, side) for c in chunks_of(r) for side in (K_SIDE, V_SIDE)]
+            for c, side in sorted(banks, key=lambda bank: not takes_detour(*bank)):
+                project(c, side)
+                if takes_detour(c, side):
+                    sums = by_round.tile([P, E, PACK], F32, tag="detour_sums")
+                    nc.scalar.copy(out=sums[:], in_=projections[c, side][:].rearrange("m j n -> m n j"))
+                    detour_sums[c, side] = sums
+
+        def add_bias_round(r):
+            grouped = by_round.tile([P, ROUND, 2, E, PACK], BF16, align_bytes=64, tag="kv_grouped", bufs=1)
+            for i, c in enumerate(chunks_of(r)):
+                for side in (K_SIDE, V_SIDE):
+                    if takes_detour(c, side):
+                        nc.gpsimd.tensor_tensor(
+                            out=grouped[:, i, side],
+                            in0=detour_sums[c, side][:],
+                            in1=bias_grouped[:, side],
+                            op=ADD,
+                        )
+                    else:
+                        nc.vector.tensor_tensor(
+                            out=grouped[:, i, side],
+                            in0=projections[c, side][:].rearrange("m j n -> m n j"),
+                            in1=bias_grouped[:, side],
+                            op=ADD,
+                        )
+            kv_grouped[r] = grouped
+
+        def quantise_kv_round(r):
+            codes = by_round.tile([P, ROUND, 2 * E], U32, align_bytes=64, tag="kv_codes")
+            scales = by_round.tile([P, ROUND, 2 * E], U8, align_bytes=64, tag="kv_scales")
             nc.vector.quantize_mx(
-                out=codes[:].bitcast(FP8X4),
-                scales=scales[:],
-                in_=kv_grouped[c][:].rearrange("m s n j -> m (s n j)"),
+                out=codes[:].rearrange("m i n -> m (i n)").bitcast(FP8X4),
+                scales=scales[:].rearrange("m i n -> m (i n)"),
+                in_=kv_grouped[r][:].rearrange("m i s n j -> m (i s n j)"),
             )
-            kv_quantised[c] = (codes, scales)
+            kv_quantised[r] = (codes, scales)
 
-        def add_to_state(c):
-            codes, scales = kv_quantised[c]
-            b, i = divmod(c, CHUNKS_PER_BATCH)
-            nc.tensor.matmul_mx(
-                out=state[:, b, :],
-                lhsT=codes[:, 0:E].bitcast(FP8X4),
-                lhsT_scale=scales[:, 0:E],
-                rhs=codes[:, E : 2 * E].bitcast(FP8X4),
-                rhs_scale=scales[:, E : 2 * E],
-                start=(i == 0),
-                stop=(i == CHUNKS_PER_BATCH - 1),
-            )
+        def add_to_state_round(r):
+            codes, scales = kv_quantised[r]
+            for i, c in enumerate(chunks_of(r)):
+                b, chunk_in_batch = divmod(c, CHUNKS_PER_BATCH)
+                nc.tensor.matmul_mx(
+                    out=state[:, b, :],
+                    lhsT=codes[:, i, 0:E].bitcast(FP8X4),
+                    lhsT_scale=scales[:, i, 0:E],
+                    rhs=codes[:, i, E : 2 * E].bitcast(FP8X4),
+                    rhs_scale=scales[:, i, E : 2 * E],
+                    start=(chunk_in_batch == 0),
+                    stop=(chunk_in_batch == CHUNKS_PER_BATCH - 1),
+                )
 
-        def in_range(c):
-            return 0 <= c < N_CHUNKS
+        def in_range(r):
+            return 0 <= r < N_ROUNDS
 
-        for t in range(N_CHUNKS + LAG_STATE):
+        for t in range(N_ROUNDS + LAG_STATE):
             if in_range(t - LAG_BIAS):
-                add_bias(t - LAG_BIAS)
+                add_bias_round(t - LAG_BIAS)
             if in_range(t - LAG_PROJECT):
-                project(t - LAG_PROJECT)
+                project_round(t - LAG_PROJECT)
             if in_range(t - LAG_QUANTISE_X):
-                quantise_x(t - LAG_QUANTISE_X)
+                quantise_x((t - LAG_QUANTISE_X) * ROUND)
             if in_range(t - LAG_BIAS):
-                quantise_kv(t - LAG_BIAS)
+                quantise_kv_round(t - LAG_BIAS)
+            if in_range(t - LAG_QUANTISE_X):
+                quantise_x((t - LAG_QUANTISE_X) * ROUND + 1)
             if in_range(t - LAG_STATE):
-                add_to_state(t - LAG_STATE)
+                add_to_state_round(t - LAG_STATE)
             if in_range(t):
-                transpose_x(t)
+                for c in chunks_of(t):
+                    transpose_x(c)
 
         result = const.tile([P, B, E], F32)
         nc.vector.tensor_copy(out=result[:], in_=state[:])

@@ -210,11 +210,10 @@ def tile_linearattention_pa_t_kernel(tc, hidden_states, Wk, bk, Wv, bv, out):
             if in_range(t - LAG_PROJECT):
                 project_round(t - LAG_PROJECT)
             if in_range(t - LAG_QUANTISE_X):
-                quantise_x((t - LAG_QUANTISE_X) * ROUND)
+                for c in chunks_of(t - LAG_QUANTISE_X):
+                    quantise_x(c)
             if in_range(t - LAG_BIAS):
                 quantise_kv_round(t - LAG_BIAS)
-            if in_range(t - LAG_QUANTISE_X):
-                quantise_x((t - LAG_QUANTISE_X) * ROUND + 1)
             if in_range(t - LAG_STATE):
                 add_to_state_round(t - LAG_STATE)
             if in_range(t):

@@ -97,6 +97,7 @@ def tile_linearattention_pa_t_kernel(tc, hidden_states, Wk, bk, Wv, bv, out):
         )
 
         state = state_psum.tile([P, B, E], F32)
+        result = const.tile([P, B, E], F32)
 
         x_grouped = {}
         x_quantised = {}
@@ -200,6 +201,9 @@ def tile_linearattention_pa_t_kernel(tc, hidden_states, Wk, bk, Wv, bv, out):
                     start=(chunk_in_batch == 0),
                     stop=(chunk_in_batch == CHUNKS_PER_BATCH - 1),
                 )
+                if chunk_in_batch == CHUNKS_PER_BATCH - 1:
+                    nc.scalar.copy(out=result[:, b, :], in_=state[:, b, :])
+                    nc.sync.dma_start(out=out[b, 0], in_=result[:, b, :])
 
         def in_range(r):
             return 0 <= r < N_ROUNDS
@@ -210,16 +214,13 @@ def tile_linearattention_pa_t_kernel(tc, hidden_states, Wk, bk, Wv, bv, out):
             if in_range(t - LAG_PROJECT):
                 project_round(t - LAG_PROJECT)
             if in_range(t - LAG_QUANTISE_X):
-                for c in chunks_of(t - LAG_QUANTISE_X):
-                    quantise_x(c)
+                quantise_x((t - LAG_QUANTISE_X) * ROUND)
             if in_range(t - LAG_BIAS):
                 quantise_kv_round(t - LAG_BIAS)
+            if in_range(t - LAG_QUANTISE_X):
+                quantise_x((t - LAG_QUANTISE_X) * ROUND + 1)
             if in_range(t - LAG_STATE):
                 add_to_state_round(t - LAG_STATE)
             if in_range(t):
                 for c in chunks_of(t):
                     transpose_x(c)
-
-        result = const.tile([P, B, E], F32)
-        nc.vector.tensor_copy(out=result[:], in_=state[:])
-        nc.sync.dma_start(out=out.rearrange("b o d e -> d (b o) e"), in_=result[:])

@@ -25,10 +25,12 @@ FLOPS = 2 * B * S * H * 2 * E + 2 * B * S * E * E
 
 ROUND = 2
 N_ROUNDS = N_CHUNKS // ROUND
+ROUNDS_PER_BATCH = CHUNKS_PER_BATCH // ROUND
 LAG_QUANTISE_X = 1
 LAG_PROJECT = 2
 LAG_BIAS = 3
 LAG_STATE = 4
+KEPT_ROUNDS = ROUNDS_PER_BATCH + 2
 
 
 def tile_linearattention_pa_t_kernel(tc, hidden_states, Wk, bk, Wv, bv, out):
@@ -41,9 +43,8 @@ def tile_linearattention_pa_t_kernel(tc, hidden_states, Wk, bk, Wv, bv, out):
         x_pool = ctx.enter_context(tc.tile_pool(name="x", bufs=N_CHUNKS))
         by_chunk = ctx.enter_context(tc.tile_pool(name="by_chunk", bufs=2 * ROUND))
         by_round = ctx.enter_context(tc.tile_pool(name="by_round", bufs=2))
-        xt_psum = ctx.enter_context(tc.psum_pool(name="xt_psum", bufs=3))
+        xt_psum = ctx.enter_context(tc.psum_pool(name="xt_psum", bufs=4))
         proj_psum = ctx.enter_context(tc.psum_pool(name="proj_psum", bufs=4))
-        state_psum = ctx.enter_context(tc.psum_pool(name="state_psum", bufs=1))
         ctx.enter_context(tc.manual_schedule())
 
         w_raw = const.tile([P, 2, PACK, E], BF16)
@@ -96,7 +97,6 @@ def tile_linearattention_pa_t_kernel(tc, hidden_states, Wk, bk, Wv, bv, out):
             in_=w_grouped[:].rearrange("q s n t -> q (s n t)"),
         )
 
-        state = state_psum.tile([P, B, E], F32)
         result = const.tile([P, B, E], F32)
 
         x_grouped = {}
@@ -105,6 +105,8 @@ def tile_linearattention_pa_t_kernel(tc, hidden_states, Wk, bk, Wv, bv, out):
         detour_sums = {}
         kv_grouped = {}
         kv_quantised = {}
+        waiting_rounds = []
+        states = {}
 
         def chunks_of(r):
             return range(r * ROUND, (r + 1) * ROUND)
@@ -117,7 +119,7 @@ def tile_linearattention_pa_t_kernel(tc, hidden_states, Wk, bk, Wv, bv, out):
             grouped = by_chunk.tile([P, PACK * P * PACK], BF16, align_bytes=64, tag="x_grouped")
             grouped_words = grouped[:].bitcast(F32).rearrange("q (j m u) -> q j m u", j=PACK, u=2)
             for half in range(2):
-                xt = xt_psum.tile([P, 2, 2, P], F32)
+                xt = xt_psum.tile([P, 2, 2, P], F32, tag="xt")
                 for j2 in range(2):
                     for u in range(2):
                         first = (2 * half + j2) * H_WORDS + u * P
@@ -179,8 +181,8 @@ def tile_linearattention_pa_t_kernel(tc, hidden_states, Wk, bk, Wv, bv, out):
             kv_grouped[r] = grouped
 
         def quantise_kv_round(r):
-            codes = by_round.tile([P, ROUND, 2 * E], U32, align_bytes=64, tag="kv_codes")
-            scales = by_round.tile([P, ROUND, 2 * E], U8, align_bytes=64, tag="kv_scales")
+            codes = by_round.tile([P, ROUND, 2 * E], U32, align_bytes=64, tag="kv_codes", bufs=KEPT_ROUNDS)
+            scales = by_round.tile([P, ROUND, 2 * E], U8, align_bytes=64, tag="kv_scales", bufs=KEPT_ROUNDS)
             nc.vector.quantize_mx(
                 out=codes[:].rearrange("m i n -> m (i n)").bitcast(FP8X4),
                 scales=scales[:].rearrange("m i n -> m (i n)"),
@@ -189,21 +191,31 @@ def tile_linearattention_pa_t_kernel(tc, hidden_states, Wk, bk, Wv, bv, out):
             kv_quantised[r] = (codes, scales)
 
         def add_to_state_round(r):
-            codes, scales = kv_quantised[r]
-            for i, c in enumerate(chunks_of(r)):
-                b, chunk_in_batch = divmod(c, CHUNKS_PER_BATCH)
-                nc.tensor.matmul_mx(
-                    out=state[:, b, :],
-                    lhsT=codes[:, i, 0:E].bitcast(FP8X4),
-                    lhsT_scale=scales[:, i, 0:E],
-                    rhs=codes[:, i, E : 2 * E].bitcast(FP8X4),
-                    rhs_scale=scales[:, i, E : 2 * E],
-                    start=(chunk_in_batch == 0),
-                    stop=(chunk_in_batch == CHUNKS_PER_BATCH - 1),
-                )
-                if chunk_in_batch == CHUNKS_PER_BATCH - 1:
-                    nc.scalar.copy(out=result[:, b, :], in_=state[:, b, :])
-                    nc.sync.dma_start(out=out[b, 0], in_=result[:, b, :])
+            waiting_rounds.append(r)
+            b, round_in_batch = divmod(r, ROUNDS_PER_BATCH)
+            complete = round_in_batch == ROUNDS_PER_BATCH - 1
+            if not complete and r != N_ROUNDS - 2:
+                return
+            for w in waiting_rounds:
+                codes, scales = kv_quantised[w]
+                for i, c in enumerate(chunks_of(w)):
+                    chunk_in_batch = c % CHUNKS_PER_BATCH
+                    if chunk_in_batch == 0:
+                        state_bank = xt_psum.tile([P, 2, 2, P], F32, tag="xt")
+                        states[b] = state_bank[:, 0, 0, :]
+                    nc.tensor.matmul_mx(
+                        out=states[b],
+                        lhsT=codes[:, i, 0:E].bitcast(FP8X4),
+                        lhsT_scale=scales[:, i, 0:E],
+                        rhs=codes[:, i, E : 2 * E].bitcast(FP8X4),
+                        rhs_scale=scales[:, i, E : 2 * E],
+                        start=(chunk_in_batch == 0),
+                        stop=(chunk_in_batch == CHUNKS_PER_BATCH - 1),
+                    )
+            waiting_rounds.clear()
+            if complete:
+                nc.scalar.copy(out=result[:, b, :], in_=states[b])
+                nc.sync.dma_start(out=out[b, 0], in_=result[:, b, :])
 
         def in_range(r):
             return 0 <= r < N_ROUNDS

@@ -9,6 +9,7 @@ U32 = mybir.dt.uint32
 U8 = mybir.dt.uint8
 FP8X4 = mybir.dt.float8_e4m3fn_x4
 ADD = mybir.AluOpType.add
+IDENTITY = mybir.ActivationFunctionType.Identity
 
 P = 128
 PACK = 4
@@ -76,9 +77,9 @@ def tile_linearattention_pa_t_kernel(tc, hidden_states, Wk, bk, Wv, bv, out):
         w_grouped = const.tile([P, 2, E, PACK], BF16, align_bytes=64)
         nc.vector.tensor_copy(out=w_grouped[:], in_=w_raw[:].rearrange("q s t n -> q s n t"))
 
-        bias_bank = proj_psum.tile([P, 2, E], F32, tag="proj")
+        bias_bank = proj_psum.tile([P, PACK, E], F32, tag="proj")
         nc.tensor.matmul(
-            out=bias_bank[:].rearrange("m s n -> m (s n)"),
+            out=bias_bank[:, 0:2].rearrange("m s n -> m (s n)"),
             lhsT=ones[:],
             rhs=bias_rows[:].rearrange("r s n -> r (s n)"),
             start=True,
@@ -86,8 +87,18 @@ def tile_linearattention_pa_t_kernel(tc, hidden_states, Wk, bk, Wv, bv, out):
         )
         bias_grouped = const.tile([P, 2, E, PACK], F32)
         nc.vector.tensor_copy(
-            out=bias_grouped[:], in_=bias_bank[:].unsqueeze(3).to_broadcast([P, 2, E, PACK])
+            out=bias_grouped[:], in_=bias_bank[:, 0:2].unsqueeze(3).to_broadcast([P, 2, E, PACK])
         )
+        for side in (K_SIDE, V_SIDE):
+            nc.tensor.matmul(
+                out=bias_bank[:, 2 + side, 0:32],
+                lhsT=bias_rows[:, side, :],
+                rhs=ones[:, 0:32],
+                start=True,
+                stop=True,
+            )
+        bias_column = const.tile([P, 2, 1], F32)
+        nc.vector.tensor_copy(out=bias_column[:], in_=bias_bank[:, 2:4, 0:1])
 
         w_codes = const.tile([P, 2 * E], U32, align_bytes=64)
         w_scales = const.tile([P, 2 * E], U8, align_bytes=64)
@@ -103,6 +114,7 @@ def tile_linearattention_pa_t_kernel(tc, hidden_states, Wk, bk, Wv, bv, out):
         x_quantised = {}
         projections = {}
         detour_sums = {}
+        turned_sums = {}
         kv_grouped = {}
         kv_quantised = {}
         waiting_rounds = []
@@ -113,6 +125,9 @@ def tile_linearattention_pa_t_kernel(tc, hidden_states, Wk, bk, Wv, bv, out):
 
         def takes_detour(c, side):
             return c % ROUND == ROUND - 1 and side == V_SIDE
+
+        def is_turned(c, side):
+            return c % (2 * ROUND) == ROUND and side == K_SIDE
 
         def transpose_x(c):
             words = x_chunks[c][:].bitcast(F32)
@@ -138,7 +153,7 @@ def tile_linearattention_pa_t_kernel(tc, hidden_states, Wk, bk, Wv, bv, out):
 
         def project(c, side):
             codes, scales = x_quantised[c]
-            proj = proj_psum.tile([P, PACK, E], F32)
+            proj = proj_psum.tile([P, PACK, E], F32, tag="proj")
             for j in range(PACK):
                 nc.tensor.matmul_mx(
                     out=proj[:, j, :],
@@ -151,9 +166,53 @@ def tile_linearattention_pa_t_kernel(tc, hidden_states, Wk, bk, Wv, bv, out):
                 )
             projections[c, side] = proj
 
+        def project_turned(c, side):
+            codes, scales = x_quantised[c]
+            proj = proj_psum.tile([P, PACK, P], F32, tag="proj")
+            nc.tensor.matmul_mx(
+                out=proj[:].rearrange("n j m -> n (j m)"),
+                lhsT=w_codes[:, side * E : (side + 1) * E].bitcast(FP8X4),
+                lhsT_scale=w_scales[:, side * E : (side + 1) * E],
+                rhs=codes[:].bitcast(FP8X4),
+                rhs_scale=scales[:],
+                start=True,
+                stop=True,
+            )
+            turned = by_round.tile([P, 2, P, 2], BF16, align_bytes=64, tag="turned")
+            nc.scalar.activation(
+                out=turned[:],
+                in_=proj[:].rearrange("n (u i) m -> n u m i", u=2),
+                func=IDENTITY,
+                bias=bias_column[:, side],
+            )
+            turned_sums[c, side] = turned
+
+        def turn_back_round(r):
+            for i, c in enumerate(chunks_of(r)):
+                for side in (K_SIDE, V_SIDE):
+                    if is_turned(c, side):
+                        words = turned_sums[c, side][:].rearrange("n u m i -> n (u m i)").bitcast(F32)
+                        back = xt_psum.tile([P, 2, 2, P], F32, tag="xt")
+                        for u in range(2):
+                            nc.tensor.transpose(back[:, 0, u, :], words[:, u * P : (u + 1) * P], identity[:])
+                        grouped_words = grouped_of(r)[:, i, side].rearrange("m n j -> m (n j)").bitcast(F32)
+                        nc.scalar.copy(
+                            out=grouped_words.rearrange("m (n u) -> m n u", u=2),
+                            in_=back[:, 0].rearrange("m u n -> m n u"),
+                        )
+
+        def grouped_of(r):
+            if r not in kv_grouped:
+                grouped = by_round.tile([P, ROUND, 2, E, PACK], BF16, align_bytes=64, tag="kv_grouped", bufs=1)
+                kv_grouped[r] = grouped
+            return kv_grouped[r]
+
         def project_round(r):
             banks = [(c, side) for c in chunks_of(r) for side in (K_SIDE, V_SIDE)]
-            for c, side in sorted(banks, key=lambda bank: not takes_detour(*bank)):
+            for c, side in sorted(banks, key=lambda bank: (not takes_detour(*bank), not is_turned(*bank))):
+                if is_turned(c, side):
+                    project_turned(c, side)
+                    continue
                 project(c, side)
                 if takes_detour(c, side):
                     sums = by_round.tile([P, E, PACK], F32, tag="detour_sums")
@@ -161,9 +220,11 @@ def tile_linearattention_pa_t_kernel(tc, hidden_states, Wk, bk, Wv, bv, out):
                     detour_sums[c, side] = sums
 
         def add_bias_round(r):
-            grouped = by_round.tile([P, ROUND, 2, E, PACK], BF16, align_bytes=64, tag="kv_grouped", bufs=1)
+            grouped = grouped_of(r)
             for i, c in enumerate(chunks_of(r)):
                 for side in (K_SIDE, V_SIDE):
+                    if is_turned(c, side):
+                        continue
                     if takes_detour(c, side):
                         nc.gpsimd.tensor_tensor(
                             out=grouped[:, i, side],
@@ -178,7 +239,6 @@ def tile_linearattention_pa_t_kernel(tc, hidden_states, Wk, bk, Wv, bv, out):
                             in1=bias_grouped[:, side],
                             op=ADD,
                         )
-            kv_grouped[r] = grouped
 
         def quantise_kv_round(r):
             codes = by_round.tile([P, ROUND, 2 * E], U32, align_bytes=64, tag="kv_codes", bufs=KEPT_ROUNDS)
@@ -233,6 +293,8 @@ def tile_linearattention_pa_t_kernel(tc, hidden_states, Wk, bk, Wv, bv, out):
                 quantise_x((t - LAG_QUANTISE_X) * ROUND + 1)
             if in_range(t - LAG_STATE):
                 add_to_state_round(t - LAG_STATE)
-            if in_range(t):
-                for c in chunks_of(t):
-                    transpose_x(c)
+            for i in range(ROUND):
+                if in_range(t):
+                    transpose_x(t * ROUND + i)
+                if i == 0 and in_range(t - LAG_PROJECT):
+                    turn_back_round(t - LAG_PROJECT)

@@ -207,9 +207,10 @@ def tile_linearattention_pa_t_kernel(tc, hidden_states, Wk, bk, Wv, bv, out):
                 kv_grouped[r] = grouped
             return kv_grouped[r]
 
-        def project_round(r):
+        def project_half(r, half):
             banks = [(c, side) for c in chunks_of(r) for side in (K_SIDE, V_SIDE)]
-            for c, side in sorted(banks, key=lambda bank: (not takes_detour(*bank), not is_turned(*bank))):
+            ordered = sorted(banks, key=lambda bank: (not takes_detour(*bank), not is_turned(*bank)))
+            for c, side in ordered[2 * half : 2 * half + 2]:
                 if is_turned(c, side):
                     project_turned(c, side)
                     continue
@@ -284,7 +285,11 @@ def tile_linearattention_pa_t_kernel(tc, hidden_states, Wk, bk, Wv, bv, out):
             if in_range(t - LAG_BIAS):
                 add_bias_round(t - LAG_BIAS)
             if in_range(t - LAG_PROJECT):
-                project_round(t - LAG_PROJECT)
+                project_half(t - LAG_PROJECT, 0)
+            if in_range(t):
+                transpose_x(t * ROUND)
+            if in_range(t - LAG_PROJECT):
+                project_half(t - LAG_PROJECT, 1)
             if in_range(t - LAG_QUANTISE_X):
                 quantise_x((t - LAG_QUANTISE_X) * ROUND)
             if in_range(t - LAG_BIAS):
@@ -293,8 +298,7 @@ def tile_linearattention_pa_t_kernel(tc, hidden_states, Wk, bk, Wv, bv, out):
                 quantise_x((t - LAG_QUANTISE_X) * ROUND + 1)
             if in_range(t - LAG_STATE):
                 add_to_state_round(t - LAG_STATE)
-            for i in range(ROUND):
-                if in_range(t):
-                    transpose_x(t * ROUND + i)
-                if i == 0 and in_range(t - LAG_PROJECT):
-                    turn_back_round(t - LAG_PROJECT)
+            if in_range(t - LAG_PROJECT):
+                turn_back_round(t - LAG_PROJECT)
+            if in_range(t):
+                transpose_x(t * ROUND + 1)

@@ -31,6 +31,7 @@ LAG_QUANTISE_X = 1
 LAG_PROJECT = 2
 LAG_BIAS = 3
 LAG_STATE = 4
+CHUNKS_IN_HALVES = 4
 KEPT_ROUNDS = ROUNDS_PER_BATCH + 2
 
 
@@ -63,10 +64,12 @@ def tile_linearattention_pa_t_kernel(tc, hidden_states, Wk, bk, Wv, bv, out):
         x_chunks = []
         for c in range(N_CHUNKS):
             x_chunk = x_pool.tile([P, PACK * H], BF16)
-            nc.sync.dma_start(
-                out=x_chunk[:],
-                in_=x_rows[c * CHUNK : (c + 1) * CHUNK, :].rearrange("(m j) h -> m (j h)", j=PACK),
-            )
+            rows = x_rows[c * CHUNK : (c + 1) * CHUNK, :].rearrange("(m j) h -> m (j h)", j=PACK)
+            width = PACK * H // 2 if c < CHUNKS_IN_HALVES else PACK * H
+            for first in range(0, PACK * H, width):
+                nc.sync.dma_start(
+                    out=x_chunk[:, first : first + width], in_=rows[:, first : first + width]
+                )
             x_chunks.append(x_chunk)
 
         ones = const.tile([P, P], BF16)

@@ -127,10 +127,12 @@ def tile_linearattention_pa_t_kernel(tc, hidden_states, Wk, bk, Wv, bv, out):
             return range(r * ROUND, (r + 1) * ROUND)
 
         def takes_detour(c, side):
-            return c % ROUND == ROUND - 1 and side == V_SIDE
+            return c % ROUND == ROUND - 1 and side == V_SIDE and c != N_CHUNKS - 1
 
         def is_turned(c, side):
-            return c % (2 * ROUND) == ROUND and side == K_SIDE
+            if side == K_SIDE:
+                return c % (2 * ROUND) == ROUND or c == N_CHUNKS - 2 * ROUND
+            return c == N_CHUNKS - 1
 
         def transpose_x(c):
             words = x_chunks[c][:].bitcast(F32)
@@ -247,11 +249,13 @@ def tile_linearattention_pa_t_kernel(tc, hidden_states, Wk, bk, Wv, bv, out):
         def quantise_kv_round(r):
             codes = by_round.tile([P, ROUND, 2 * E], U32, align_bytes=64, tag="kv_codes", bufs=KEPT_ROUNDS)
             scales = by_round.tile([P, ROUND, 2 * E], U8, align_bytes=64, tag="kv_scales", bufs=KEPT_ROUNDS)
-            nc.vector.quantize_mx(
-                out=codes[:].rearrange("m i n -> m (i n)").bitcast(FP8X4),
-                scales=scales[:].rearrange("m i n -> m (i n)"),
-                in_=kv_grouped[r][:].rearrange("m i s n j -> m (i s n j)"),
-            )
+            width = 1 if r >= N_ROUNDS - 2 else ROUND
+            for i in range(0, ROUND, width):
+                nc.vector.quantize_mx(
+                    out=codes[:, i : i + width].rearrange("m i n -> m (i n)").bitcast(FP8X4),
+                    scales=scales[:, i : i + width].rearrange("m i n -> m (i n)"),
+                    in_=kv_grouped[r][:, i : i + width].rearrange("m i s n j -> m (i s n j)"),
+                )
             kv_quantised[r] = (codes, scales)
 
         def add_to_state_round(r):

@@ -32,6 +32,8 @@ LAG_PROJECT = 2
 LAG_BIAS = 3
 LAG_STATE = 4
 CHUNKS_IN_HALVES = 4
+WARM_PRODUCTS = 6
+WARM_COLUMNS = 384
 KEPT_ROUNDS = ROUNDS_PER_BATCH + 2
 
 
@@ -72,10 +74,24 @@ def tile_linearattention_pa_t_kernel(tc, hidden_states, Wk, bk, Wv, bv, out):
                 )
             x_chunks.append(x_chunk)
 
-        ones = const.tile([P, P], BF16)
+        ones = const.tile([P, PACK * E], BF16)
         nc.vector.memset(ones[:], 1.0)
         identity = const.tile([P, P], F32)
         make_identity(nc, identity[:])
+
+        warm_bank = proj_psum.tile([P, PACK * E], F32, tag="proj")
+
+        def keep_clock_up(columns):
+            nc.tensor.matmul(
+                out=warm_bank[:, 0:columns],
+                lhsT=ones[:, 0:P],
+                rhs=ones[:, 0:columns],
+                start=True,
+                stop=True,
+            )
+
+        for i in range(WARM_PRODUCTS):
+            keep_clock_up(PACK * E)
 
         w_grouped = const.tile([P, 2, E, PACK], BF16, align_bytes=64)
         nc.vector.tensor_copy(out=w_grouped[:], in_=w_raw[:].rearrange("q s t n -> q s n t"))
@@ -83,7 +99,7 @@ def tile_linearattention_pa_t_kernel(tc, hidden_states, Wk, bk, Wv, bv, out):
         bias_bank = proj_psum.tile([P, PACK, E], F32, tag="proj")
         nc.tensor.matmul(
             out=bias_bank[:, 0:2].rearrange("m s n -> m (s n)"),
-            lhsT=ones[:],
+            lhsT=ones[:, 0:P],
             rhs=bias_rows[:].rearrange("r s n -> r (s n)"),
             start=True,
             stop=True,
@@ -144,6 +160,8 @@ def tile_linearattention_pa_t_kernel(tc, hidden_states, Wk, bk, Wv, bv, out):
                     for u in range(2):
                         first = (2 * half + j2) * H_WORDS + u * P
                         nc.tensor.transpose(xt[:, j2, u, :], words[:, first : first + P], identity[:])
+                if c < LAG_PROJECT * ROUND:
+                    keep_clock_up(WARM_COLUMNS)
                 nc.scalar.copy(
                     out=grouped_words[:, 2 * half : 2 * half + 2],
                     in_=xt[:].rearrange("q j u m -> q j m u"),

@@ -32,7 +32,7 @@ LAG_PROJECT = 2
 LAG_BIAS = 3
 LAG_STATE = 4
 CHUNKS_IN_HALVES = 4
-WARM_PRODUCTS = 6
+WARM_PRODUCTS = 5
 WARM_COLUMNS = 384
 KEPT_ROUNDS = ROUNDS_PER_BATCH + 2
 
@@ -50,6 +50,9 @@ def tile_linearattention_pa_t_kernel(tc, hidden_states, Wk, bk, Wv, bv, out):
         xt_psum = ctx.enter_context(tc.psum_pool(name="xt_psum", bufs=4))
         proj_psum = ctx.enter_context(tc.psum_pool(name="proj_psum", bufs=4))
         ctx.enter_context(tc.manual_schedule())
+
+        ones = const.tile([P, PACK * E], BF16)
+        nc.vector.memset(ones[:], 1.0)
 
         w_raw = const.tile([P, 2, PACK, E], BF16)
         for side, w in ((K_SIDE, Wk), (V_SIDE, Wv)):
@@ -74,8 +77,6 @@ def tile_linearattention_pa_t_kernel(tc, hidden_states, Wk, bk, Wv, bv, out):
                 )
             x_chunks.append(x_chunk)
 
-        ones = const.tile([P, PACK * E], BF16)
-        nc.vector.memset(ones[:], 1.0)
         identity = const.tile([P, P], F32)
         make_identity(nc, identity[:])
 

@@ -33,7 +33,6 @@ LAG_BIAS = 3
 LAG_STATE = 4
 CHUNKS_IN_HALVES = 4
 WARM_PRODUCTS = 5
-WARM_COLUMNS = 384
 KEPT_ROUNDS = ROUNDS_PER_BATCH + 2
 
 
@@ -82,17 +81,17 @@ def tile_linearattention_pa_t_kernel(tc, hidden_states, Wk, bk, Wv, bv, out):
 
         warm_bank = proj_psum.tile([P, PACK * E], F32, tag="proj")
 
-        def keep_clock_up(columns):
+        def keep_clock_up():
             nc.tensor.matmul(
-                out=warm_bank[:, 0:columns],
+                out=warm_bank[:],
                 lhsT=ones[:, 0:P],
-                rhs=ones[:, 0:columns],
+                rhs=ones[:],
                 start=True,
                 stop=True,
             )
 
         for i in range(WARM_PRODUCTS):
-            keep_clock_up(PACK * E)
+            keep_clock_up()
 
         w_grouped = const.tile([P, 2, E, PACK], BF16, align_bytes=64)
         nc.vector.tensor_copy(out=w_grouped[:], in_=w_raw[:].rearrange("q s t n -> q s n t"))
@@ -161,8 +160,8 @@ def tile_linearattention_pa_t_kernel(tc, hidden_states, Wk, bk, Wv, bv, out):
                     for u in range(2):
                         first = (2 * half + j2) * H_WORDS + u * P
                         nc.tensor.transpose(xt[:, j2, u, :], words[:, first : first + P], identity[:])
-                if c < LAG_PROJECT * ROUND:
-                    keep_clock_up(WARM_COLUMNS)
+                if c < LAG_PROJECT * ROUND and half == 0:
+                    keep_clock_up()
                 nc.scalar.copy(
                     out=grouped_words[:, 2 * half : 2 * half + 2],
                     in_=xt[:].rearrange("q j u m -> q j m u"),

from contextlib import ExitStack

import concourse.mybir as mybir
from concourse.masks import make_identity

BF16 = mybir.dt.bfloat16
F32 = mybir.dt.float32
U32 = mybir.dt.uint32
U8 = mybir.dt.uint8
FP8X4 = mybir.dt.float8_e4m3fn_x4
ADD = mybir.AluOpType.add
IDENTITY = mybir.ActivationFunctionType.Identity

P = 128
PACK = 4
K_PASS = P * PACK

B, S, H, E = 4, 4096, 512, 128
CHUNK = K_PASS
CHUNKS_PER_BATCH = S // CHUNK
N_CHUNKS = B * CHUNKS_PER_BATCH
H_WORDS = H // 2
K_SIDE, V_SIDE = 0, 1

FLOPS = 2 * B * S * H * 2 * E + 2 * B * S * E * E

ROUND = 2
N_ROUNDS = N_CHUNKS // ROUND
ROUNDS_PER_BATCH = CHUNKS_PER_BATCH // ROUND
LAG_QUANTISE_X = 1
LAG_PROJECT = 2
LAG_BIAS = 3
LAG_STATE = 4
CHUNKS_IN_HALVES = 4
WARM_PRODUCTS = 5
KEPT_ROUNDS = ROUNDS_PER_BATCH + 2


def tile_linearattention_pa_t_kernel(tc, hidden_states, Wk, bk, Wv, bv, out):
    nc = tc.nc
    assert H == K_PASS, "the first contraction is exactly one matmul_mx pass"
    x_rows = hidden_states.flatten_outer_dims()

    with ExitStack() as ctx:
        const = ctx.enter_context(tc.tile_pool(name="const", bufs=1))
        x_pool = ctx.enter_context(tc.tile_pool(name="x", bufs=N_CHUNKS))
        by_chunk = ctx.enter_context(tc.tile_pool(name="by_chunk", bufs=2 * ROUND))
        by_round = ctx.enter_context(tc.tile_pool(name="by_round", bufs=2))
        xt_psum = ctx.enter_context(tc.psum_pool(name="xt_psum", bufs=4))
        proj_psum = ctx.enter_context(tc.psum_pool(name="proj_psum", bufs=4))
        ctx.enter_context(tc.manual_schedule())

        ones = const.tile([P, PACK * E], BF16)
        nc.vector.memset(ones[:], 1.0)

        w_raw = const.tile([P, 2, PACK, E], BF16)
        for side, w in ((K_SIDE, Wk), (V_SIDE, Wv)):
            nc.sync.dma_start(
                out=w_raw[:, side].rearrange("q (u e) n -> q u e n", u=2),
                in_=w.rearrange("(u q e) n -> q u e n", u=2, e=2),
            )
        bias_rows = const.tile([P, 2, E], BF16)
        nc.vector.memset(bias_rows[:], 0.0)
        for side, bias in ((K_SIDE, bk), (V_SIDE, bv)):
            nc.sync.dma_start(
                out=bias_rows[0:1, side, :], in_=bias.rearrange("(o n) -> o n", o=1)
            )
        x_chunks = []
        for c in range(N_CHUNKS):
            x_chunk = x_pool.tile([P, PACK * H], BF16)
            rows = x_rows[c * CHUNK : (c + 1) * CHUNK, :].rearrange("(m j) h -> m (j h)", j=PACK)
            width = PACK * H // 2 if c < CHUNKS_IN_HALVES else PACK * H
            for first in range(0, PACK * H, width):
                nc.sync.dma_start(
                    out=x_chunk[:, first : first + width], in_=rows[:, first : first + width]
                )
            x_chunks.append(x_chunk)

        identity = const.tile([P, P], F32)
        make_identity(nc, identity[:])

        warm_bank = proj_psum.tile([P, PACK * E], F32, tag="proj")

        def keep_clock_up():
            nc.tensor.matmul(
                out=warm_bank[:],
                lhsT=ones[:, 0:P],
                rhs=ones[:],
                start=True,
                stop=True,
            )

        for i in range(WARM_PRODUCTS):
            keep_clock_up()

        w_grouped = const.tile([P, 2, E, PACK], BF16, align_bytes=64)
        nc.vector.tensor_copy(out=w_grouped[:], in_=w_raw[:].rearrange("q s t n -> q s n t"))

        bias_bank = proj_psum.tile([P, PACK, E], F32, tag="proj")
        nc.tensor.matmul(
            out=bias_bank[:, 0:2].rearrange("m s n -> m (s n)"),
            lhsT=ones[:, 0:P],
            rhs=bias_rows[:].rearrange("r s n -> r (s n)"),
            start=True,
            stop=True,
        )
        bias_grouped = const.tile([P, 2, E, PACK], F32)
        nc.vector.tensor_copy(
            out=bias_grouped[:], in_=bias_bank[:, 0:2].unsqueeze(3).to_broadcast([P, 2, E, PACK])
        )
        for side in (K_SIDE, V_SIDE):
            nc.tensor.matmul(
                out=bias_bank[:, 2 + side, 0:32],
                lhsT=bias_rows[:, side, :],
                rhs=ones[:, 0:32],
                start=True,
                stop=True,
            )
        bias_column = const.tile([P, 2, 1], F32)
        nc.vector.tensor_copy(out=bias_column[:], in_=bias_bank[:, 2:4, 0:1])

        w_codes = const.tile([P, 2 * E], U32, align_bytes=64)
        w_scales = const.tile([P, 2 * E], U8, align_bytes=64)
        nc.vector.quantize_mx(
            out=w_codes[:].bitcast(FP8X4),
            scales=w_scales[:],
            in_=w_grouped[:].rearrange("q s n t -> q (s n t)"),
        )

        result = const.tile([P, B, E], F32)

        x_grouped = {}
        x_quantised = {}
        projections = {}
        detour_sums = {}
        turned_sums = {}
        kv_grouped = {}
        kv_quantised = {}
        waiting_rounds = []
        states = {}

        def chunks_of(r):
            return range(r * ROUND, (r + 1) * ROUND)

        def takes_detour(c, side):
            return c % ROUND == ROUND - 1 and side == V_SIDE and c != N_CHUNKS - 1

        def is_turned(c, side):
            if side == K_SIDE:
                return c % (2 * ROUND) == ROUND or c == N_CHUNKS - 2 * ROUND
            return c == N_CHUNKS - 1

        def transpose_x(c):
            words = x_chunks[c][:].bitcast(F32)
            grouped = by_chunk.tile([P, PACK * P * PACK], BF16, align_bytes=64, tag="x_grouped")
            grouped_words = grouped[:].bitcast(F32).rearrange("q (j m u) -> q j m u", j=PACK, u=2)
            for half in range(2):
                xt = xt_psum.tile([P, 2, 2, P], F32, tag="xt")
                for j2 in range(2):
                    for u in range(2):
                        first = (2 * half + j2) * H_WORDS + u * P
                        nc.tensor.transpose(xt[:, j2, u, :], words[:, first : first + P], identity[:])
                if c < LAG_PROJECT * ROUND and half == 0:
                    keep_clock_up()
                nc.scalar.copy(
                    out=grouped_words[:, 2 * half : 2 * half + 2],
                    in_=xt[:].rearrange("q j u m -> q j m u"),
                )
            x_grouped[c] = grouped

        def quantise_x(c):
            codes = by_chunk.tile([P, PACK * P], U32, align_bytes=64, tag="x_codes")
            scales = by_chunk.tile([P, PACK * P], U8, align_bytes=64, tag="x_scales")
            nc.vector.quantize_mx(out=codes[:].bitcast(FP8X4), scales=scales[:], in_=x_grouped[c][:])
            x_quantised[c] = (codes, scales)

        def project(c, side):
            codes, scales = x_quantised[c]
            proj = proj_psum.tile([P, PACK, E], F32, tag="proj")
            for j in range(PACK):
                nc.tensor.matmul_mx(
                    out=proj[:, j, :],
                    lhsT=codes[:, j * P : (j + 1) * P].bitcast(FP8X4),
                    lhsT_scale=scales[:, j * P : (j + 1) * P],
                    rhs=w_codes[:, side * E : (side + 1) * E].bitcast(FP8X4),
                    rhs_scale=w_scales[:, side * E : (side + 1) * E],
                    start=True,
                    stop=True,
                )
            projections[c, side] = proj

        def project_turned(c, side):
            codes, scales = x_quantised[c]
            proj = proj_psum.tile([P, PACK, P], F32, tag="proj")
            nc.tensor.matmul_mx(
                out=proj[:].rearrange("n j m -> n (j m)"),
                lhsT=w_codes[:, side * E : (side + 1) * E].bitcast(FP8X4),
                lhsT_scale=w_scales[:, side * E : (side + 1) * E],
                rhs=codes[:].bitcast(FP8X4),
                rhs_scale=scales[:],
                start=True,
                stop=True,
            )
            turned = by_round.tile([P, 2, P, 2], BF16, align_bytes=64, tag="turned")
            nc.scalar.activation(
                out=turned[:],
                in_=proj[:].rearrange("n (u i) m -> n u m i", u=2),
                func=IDENTITY,
                bias=bias_column[:, side],
            )
            turned_sums[c, side] = turned

        def turn_back_round(r):
            for i, c in enumerate(chunks_of(r)):
                for side in (K_SIDE, V_SIDE):
                    if is_turned(c, side):
                        words = turned_sums[c, side][:].rearrange("n u m i -> n (u m i)").bitcast(F32)
                        back = xt_psum.tile([P, 2, 2, P], F32, tag="xt")
                        for u in range(2):
                            nc.tensor.transpose(back[:, 0, u, :], words[:, u * P : (u + 1) * P], identity[:])
                        grouped_words = grouped_of(r)[:, i, side].rearrange("m n j -> m (n j)").bitcast(F32)
                        nc.scalar.copy(
                            out=grouped_words.rearrange("m (n u) -> m n u", u=2),
                            in_=back[:, 0].rearrange("m u n -> m n u"),
                        )

        def grouped_of(r):
            if r not in kv_grouped:
                grouped = by_round.tile([P, ROUND, 2, E, PACK], BF16, align_bytes=64, tag="kv_grouped", bufs=1)
                kv_grouped[r] = grouped
            return kv_grouped[r]

        def project_half(r, half):
            banks = [(c, side) for c in chunks_of(r) for side in (K_SIDE, V_SIDE)]
            ordered = sorted(banks, key=lambda bank: (not takes_detour(*bank), not is_turned(*bank)))
            for c, side in ordered[2 * half : 2 * half + 2]:
                if is_turned(c, side):
                    project_turned(c, side)
                    continue
                project(c, side)
                if takes_detour(c, side):
                    sums = by_round.tile([P, E, PACK], F32, tag="detour_sums")
                    nc.scalar.copy(out=sums[:], in_=projections[c, side][:].rearrange("m j n -> m n j"))
                    detour_sums[c, side] = sums

        def add_bias_round(r):
            grouped = grouped_of(r)
            for i, c in enumerate(chunks_of(r)):
                for side in (K_SIDE, V_SIDE):
                    if is_turned(c, side):
                        continue
                    if takes_detour(c, side):
                        nc.gpsimd.tensor_tensor(
                            out=grouped[:, i, side],
                            in0=detour_sums[c, side][:],
                            in1=bias_grouped[:, side],
                            op=ADD,
                        )
                    else:
                        nc.vector.tensor_tensor(
                            out=grouped[:, i, side],
                            in0=projections[c, side][:].rearrange("m j n -> m n j"),
                            in1=bias_grouped[:, side],
                            op=ADD,
                        )

        def quantise_kv_round(r):
            codes = by_round.tile([P, ROUND, 2 * E], U32, align_bytes=64, tag="kv_codes", bufs=KEPT_ROUNDS)
            scales = by_round.tile([P, ROUND, 2 * E], U8, align_bytes=64, tag="kv_scales", bufs=KEPT_ROUNDS)
            width = 1 if r >= N_ROUNDS - 2 else ROUND
            for i in range(0, ROUND, width):
                nc.vector.quantize_mx(
                    out=codes[:, i : i + width].rearrange("m i n -> m (i n)").bitcast(FP8X4),
                    scales=scales[:, i : i + width].rearrange("m i n -> m (i n)"),
                    in_=kv_grouped[r][:, i : i + width].rearrange("m i s n j -> m (i s n j)"),
                )
            kv_quantised[r] = (codes, scales)

        def add_to_state_round(r):
            waiting_rounds.append(r)
            b, round_in_batch = divmod(r, ROUNDS_PER_BATCH)
            complete = round_in_batch == ROUNDS_PER_BATCH - 1
            if not complete and r != N_ROUNDS - 2:
                return
            for w in waiting_rounds:
                codes, scales = kv_quantised[w]
                for i, c in enumerate(chunks_of(w)):
                    chunk_in_batch = c % CHUNKS_PER_BATCH
                    if chunk_in_batch == 0:
                        state_bank = xt_psum.tile([P, 2, 2, P], F32, tag="xt")
                        states[b] = state_bank[:, 0, 0, :]
                    nc.tensor.matmul_mx(
                        out=states[b],
                        lhsT=codes[:, i, 0:E].bitcast(FP8X4),
                        lhsT_scale=scales[:, i, 0:E],
                        rhs=codes[:, i, E : 2 * E].bitcast(FP8X4),
                        rhs_scale=scales[:, i, E : 2 * E],
                        start=(chunk_in_batch == 0),
                        stop=(chunk_in_batch == CHUNKS_PER_BATCH - 1),
                    )
            waiting_rounds.clear()
            if complete:
                nc.scalar.copy(out=result[:, b, :], in_=states[b])
                nc.sync.dma_start(out=out[b, 0], in_=result[:, b, :])

        def in_range(r):
            return 0 <= r < N_ROUNDS

        for t in range(N_ROUNDS + LAG_STATE):
            if in_range(t - LAG_BIAS):
                add_bias_round(t - LAG_BIAS)
            if in_range(t - LAG_PROJECT):
                project_half(t - LAG_PROJECT, 0)
            if in_range(t):
                transpose_x(t * ROUND)
            if in_range(t - LAG_PROJECT):
                project_half(t - LAG_PROJECT, 1)
            if in_range(t - LAG_QUANTISE_X):
                quantise_x((t - LAG_QUANTISE_X) * ROUND)
            if in_range(t - LAG_BIAS):
                quantise_kv_round(t - LAG_BIAS)
            if in_range(t - LAG_QUANTISE_X):
                quantise_x((t - LAG_QUANTISE_X) * ROUND + 1)
            if in_range(t - LAG_STATE):
                add_to_state_round(t - LAG_STATE)
            if in_range(t - LAG_PROJECT):
                turn_back_round(t - LAG_PROJECT)
            if in_range(t):
                transpose_x(t * ROUND + 1)
